import numpy as np
import ml_dtypes


def mxq(x, axis, fmt="e4m3"):
    dtype, down = {"e4m3": (ml_dtypes.float8_e4m3fn, 7), "e5m2": (ml_dtypes.float8_e5m2, 14)}[fmt]
    v = np.moveaxis(np.asarray(x, np.float32).astype(ml_dtypes.bfloat16).astype(np.float64), axis, -1)
    blocks = v.reshape(v.shape[:-1] + (-1, 32))
    amax = np.abs(blocks).max(-1, keepdims=True)
    byte = np.maximum(np.where(amax > 0, np.frexp(amax)[1] - 1 + 127, 0) - down, 1)
    scale = np.exp2(byte - 127.0)
    codes = (blocks / scale).astype(np.float32).astype(dtype).astype(np.float64)
    return np.moveaxis((codes * scale).reshape(v.shape), -1, axis)


WIDE = False


def mx_kscale(k):
    if not WIDE:
        return np.ones(k)
    levels = np.array([18, -18])
    if k % 512:
        return np.exp2(np.random.permutation(np.resize(levels, k // 32))).repeat(32)
    a = np.empty((k // 512, 16))
    for p in range(k // 512):
        a[p, :8] = np.random.permutation(np.resize(levels, 8))
        for g in range(8):
            far = levels[np.abs(levels - a[p, g]) >= 10]
            a[p, g + 8] = far[np.random.randint(len(far))]
    return np.exp2(a.ravel()).repeat(32)


BF16 = ml_dtypes.bfloat16


def bf(x):
    return np.asarray(x, np.float32).astype(BF16)


def f64(x):
    return np.asarray(x).astype(np.float64)


B, T, N, D = 2, 2, 512, 512


def setup_inputs():
    u = mx_kscale(D)
    v = mx_kscale(D)
    s = mx_kscale(N)
    adj0 = bf(np.random.uniform(size=(N, N)) * 16.0 / N)
    query0 = bf(np.random.standard_normal((B, T, N, D)) * 0.8)
    Wt0 = bf(np.random.standard_normal((D, D)) * 10.0 / np.sqrt(D))
    bt = bf(np.random.standard_normal(D) * 0.2)
    g = bf(np.random.standard_normal((B, T, N, D)) * np.exp2(np.random.randint(-6, 1, (B, T, N, 1))) / s[:, None] * u * np.min(s))
    A = f64(adj0) + np.eye(N)
    rdeg = 1.0 / A.sum(1)
    nadj = A * rdeg[:, None]
    z2 = (nadj @ f64(query0)) @ f64(Wt0).T + f64(bt)
    return {"adj": bf(f64(adj0) * s[:, None] / s[None, :]),
            "query": bf(f64(query0) / v),
            "Wt": bf(f64(Wt0) / u[:, None] * v[None, :]),
            "bt": bt,
            "z2": np.asarray(z2, np.float32),
            "nadj": np.asarray(nadj, np.float32),
            "rdeg": np.asarray(rdeg, np.float32),
            "grad_out": g}


def reference(adj, query, Wt, bt, z2, nadj, rdeg, grad_out):
    dz2 = f64(grad_out) * (f64(z2) > 0.0)
    dgq = mxq(dz2, 3, "e5m2") @ mxq(f64(Wt), 0, "e4m3")
    dz1 = dgq * f64(rdeg)[:, None]
    dquery = (mxq(f64(adj), 0, "e4m3").T @ mxq(dz1, 2, "e5m2")) + dz1
    dzf = dz1.transpose(2, 0, 1, 3).reshape(N, B * T * D)
    qf = f64(query).transpose(2, 0, 1, 3).reshape(N, B * T * D)
    P = mxq(dzf, 1, "e5m2") @ mxq(qf, 1, "e4m3").T
    dadj = P - (P * f64(nadj)).sum(1, keepdims=True)
    return dquery, dadj

@@ -1,0 +1,439 @@
+from contextlib import ExitStack
+
+import concourse.mybir as mybir
+from concourse.masks import make_identity
+
+F32 = mybir.dt.float32
+BF16 = mybir.dt.bfloat16
+U32 = mybir.dt.uint32
+U8 = mybir.dt.uint8
+E4M3 = mybir.dt.float8_e4m3fn_x4
+E5M2 = mybir.dt.float8_e5m2_x4
+ALU = mybir.AluOpType
+ACT = mybir.ActivationFunctionType
+
+P = 128
+PACK = 4
+W = 512
+SLABS = 4
+HALVES = 2
+BANKS = 8
+SCALAR_SHARE = [0, 24, 16, 32]
+ADJ_SHARE = 64
+
+FLOPS = 3 * 2 * SLABS * W * W * W
+BYTES = 2 * (2 * W * W + 2 * SLABS * W * W) + 4 * (SLABS * W * W + W * W + W) + 4 * (SLABS * W * W + W * W)
+
+
+def tile_gatedspatialattentionlayer_pc_v_kernel(
+    tc, adj, query, Wt, bt, z2, nadj, rdeg, grad_out, out_0, out_1
+):
+    nc = tc.nc
+    rows = "b s (p t) w -> (b s) p t w"
+    z_hbm = z2.rearrange(rows, t=PACK)
+    g_hbm = grad_out.rearrange(rows, t=PACK)
+    q_hbm = query.rearrange(rows, t=PACK)
+    o_hbm = out_0.rearrange(rows, t=PACK)
+    dadj_hbm = out_1.rearrange("(p t) m -> p t m", t=PACK)
+
+    with ExitStack() as ctx:
+        keep = ctx.enter_context(tc.tile_pool(name="keep", bufs=1))
+        stage = ctx.enter_context(tc.tile_pool(name="stage", bufs=2))
+        psum = ctx.enter_context(tc.psum_pool(name="psum", bufs=1))
+        ctx.enter_context(tc.manual_schedule())
+
+        tiles = {}
+        free_banks = list(range(BANKS))
+        bank_of = {}
+
+        def take_bank(key):
+            number = free_banks.pop(0)
+            bank_of[key] = number
+            tiles[key] = psum.tile([P, W], F32, name="%s_%d_%d" % key, tag="bank%d" % number)
+            return tiles[key]
+
+        def free_bank(key):
+            free_banks.append(bank_of[key])
+
+        def mx_tiles(pool, name, tag):
+            codes = pool.tile([P, W], U32, name=name + "_codes", tag=tag + "_codes", align_bytes=64)
+            scales = pool.tile([P, W], U8, name=name + "_scales", tag=tag + "_scales", align_bytes=64)
+            return codes, scales
+
+        def quantize(operand, fmt, values, first):
+            codes, scales = operand
+            cols = slice(first, first + values.shape[1] // PACK)
+            nc.vector.quantize_mx(out=codes[:, cols].bitcast(fmt), scales=scales[:, cols], in_=values)
+
+        def product(out, stationary, stationary_fmt, t, moving, moving_fmt, start, stop):
+            cols = slice(t * P, (t + 1) * P)
+            nc.tensor.matmul_mx(
+                out=out[:],
+                lhsT=stationary[0][:, cols].bitcast(stationary_fmt),
+                lhsT_scale=stationary[1][:, cols],
+                rhs=moving[0][:].bitcast(moving_fmt),
+                rhs_scale=moving[1][:],
+                start=start,
+                stop=stop,
+            )
+
+        def load(name, source, dtype):
+            tile = keep.tile(list(source.shape), dtype, name=name, align_bytes=64)
+            nc.sync.dma_start(out=tile[:], in_=source)
+            return tile
+
+        def load_rows(name, hbm, dtype, b, lo, hi):
+            tile = load("%s_%d_%d" % (name, b, lo), hbm[b][:, lo:hi, :], dtype)
+            for t in range(lo, hi):
+                tiles[name, b, t] = (tile, lo)
+
+        def loaded_rows(name, b, lo, hi):
+            tile, first = tiles[name, b, lo]
+            return tile[:, lo - first : hi - first, :].rearrange("p t o -> p (t o)")
+
+        def load_grad(b, lo, hi):
+            load_rows("g", g_hbm, BF16, b, lo, hi)
+            load_rows("z", z_hbm, F32, b, lo, hi)
+
+        def warm(count):
+            for n in range(count):
+                nc.tensor.matmul(tiles["warm", 0, 0][:, :P], lhsT=identity[:], rhs=identity[:], start=True, stop=True)
+
+        def load_query(b):
+            tiles["q", b] = load("q_%d" % b, q_hbm[b], BF16)
+
+        def mask(b, lo, hi):
+            dz2 = stage.tile([P, (hi - lo) * W], BF16, name="dz2_%d_%d" % (b, lo), tag="dz2", bufs=4, align_bytes=64)
+            tiles["dz2", b, lo] = dz2
+            nc.vector.scalar_tensor_tensor(
+                out=dz2[:],
+                in0=loaded_rows("z", b, lo, hi),
+                scalar=0.0,
+                in1=loaded_rows("g", b, lo, hi),
+                op0=ALU.is_gt,
+                op1=ALU.mult,
+            )
+
+        def turn_rows(key, values):
+            bank = take_bank(key)
+            words = values.bitcast(F32).rearrange("p (t w u) -> p t w u", w=P, u=2)
+            for t in range(words.shape[1]):
+                for u in range(2):
+                    at = (2 * t + u) * P
+                    nc.tensor.transpose(bank[:, at : at + P], words[:, t, :, u], identity[:])
+
+        def copy_rows(key, turned):
+            width = turned.shape[1] // 2
+            nc.scalar.copy(
+                out=turned.bitcast(F32).rearrange("w (t p u) -> w t p u", p=P, u=2),
+                in_=tiles[key][:, :width].rearrange("w (t u p) -> w t p u", p=P, u=2),
+            )
+            free_bank(key)
+
+        def turn_dz2(b, lo):
+            turn_rows(("dz2_bank", b, lo), tiles["dz2", b, lo][:])
+
+        def copy_dz2(b, lo, hi):
+            turned = stage.tile([P, (hi - lo) * W], BF16, name="dz2_t_%d_%d" % (b, lo), tag="dz2_t", bufs=4, align_bytes=64)
+            tiles["dz2_t", b, lo] = turned
+            copy_rows(("dz2_bank", b, lo), turned[:])
+
+        def quantize_dz2(b, lo):
+            if lo == 0:
+                tiles["dz2_mx", b] = mx_tiles(stage, "dz2_%d" % b, "dz2")
+            quantize(tiles["dz2_mx", b], E5M2, tiles["dz2_t", b, lo][:], lo * P)
+
+        def turn_query(b, h):
+            turn_rows(("q_bank", b, h), tiles["q", b][:].rearrange("p t d -> p (t d)")[:, h * 2 * W : (h + 1) * 2 * W])
+
+        def copy_query(b, h):
+            if h == 0:
+                tiles["q_t", b] = stage.tile([P, PACK * W], BF16, name="q_t_%d" % b, tag="q_t", bufs=3, align_bytes=64)
+            copy_rows(("q_bank", b, h), tiles["q_t", b][:, h * 2 * W : (h + 1) * 2 * W])
+
+        def quantize_query(b):
+            tiles["q_mx", b] = mx_tiles(keep, "q_%d" % b, "q_%d" % b)
+            quantize(tiles["q_mx", b], E4M3, tiles["q_t", b][:], 0)
+
+        def multiply_dgq(b, t, warmers=0):
+            bank = take_bank(("dgq", b, t))
+            for n in range(warmers):
+                nc.tensor.matmul(bank[:, :P], lhsT=identity[:], rhs=identity[:], start=True, stop=True)
+            product(bank, tiles["dz2_mx", b], E5M2, t, wt_mx, E4M3, True, True)
+
+        def scale_dgq(b, t):
+            if t == 0:
+                tiles["dz1", b] = stage.tile([P, PACK, W], F32, name="dz1_%d" % b, tag="dz1", bufs=3, align_bytes=64)
+            nc.scalar.activation(
+                out=tiles["dz1", b][:, t, :], in_=tiles["dgq", b, t][:], func=ACT.Copy, scale=rdeg_sb[:, t : t + 1]
+            )
+            free_bank(("dgq", b, t))
+
+        def round_dz1(b):
+            rounded = stage.tile([P, PACK * W], BF16, name="dz1_n_%d" % b, tag="dz1_n", align_bytes=64)
+            tiles["dz1_n", b] = rounded
+            dst = rounded[:].rearrange("p (j r t) -> p r t j", j=PACK, t=PACK)
+            src = tiles["dz1", b][:].rearrange("p t (r j) -> p r t j", j=PACK)
+            share = SCALAR_SHARE[b]
+            if share:
+                nc.scalar.copy(out=dst[:, :share], in_=src[:, :share])
+            nc.vector.tensor_copy(out=dst[:, share:], in_=src[:, share:])
+
+        def quantize_dz1_nodes(b):
+            tiles["dz1_n_mx", b] = mx_tiles(stage, "dz1_n_%d" % b, "dz1_n")
+            quantize(tiles["dz1_n_mx", b], E5M2, tiles["dz1_n", b][:], 0)
+
+        def multiply_dq(b, t):
+            product(take_bank(("dq", b, t)), adj_mx, E4M3, t, tiles["dz1_n_mx", b], E5M2, True, True)
+
+        def add_self_loop(b, t):
+            if t == 0:
+                tiles["o", b] = stage.tile([P, PACK, W], F32, name="o_%d" % b, tag="o", bufs=3)
+            nc.vector.tensor_tensor(
+                out=tiles["o", b][:, t, :].rearrange("p (r j) -> p r j", j=PACK),
+                in0=tiles["dq", b, t][:].rearrange("p (j r) -> p r j", j=PACK),
+                in1=tiles["dz1", b][:, t, :].rearrange("p (r j) -> p r j", j=PACK),
+                op=ALU.add,
+            )
+            free_bank(("dq", b, t))
+
+        def store_dq(b, lo, hi):
+            nc.sync.dma_start(out=o_hbm[b][:, lo:hi, :], in_=tiles["o", b][:, lo:hi, :])
+
+        def turn_dz1(b, u, warmers=0):
+            bank = take_bank(("dz1_bank", b, u))
+            for n in range(warmers):
+                nc.tensor.matmul(bank[:, :P], lhsT=identity[:], rhs=identity[:], start=True, stop=True)
+            words = tiles["dz1_n", b][:].bitcast(F32).rearrange("p (j r u) -> p j r u", j=PACK, u=2)
+            for j in range(PACK):
+                nc.tensor.transpose(bank[:, j * P : (j + 1) * P], words[:, j, :, u], identity[:])
+
+        def copy_dz1(b, u):
+            if u == 0:
+                tiles["dz1_d", b] = stage.tile([P, PACK * W], BF16, name="dz1_d_%d" % b, tag="dz1_d", align_bytes=64)
+            nc.scalar.copy(
+                out=tiles["dz1_d", b][:, u * 2 * W : (u + 1) * 2 * W].rearrange("r (e p j) -> r e p j", e=2, j=PACK),
+                in_=tiles["dz1_bank", b, u][:].bitcast(BF16).rearrange("r (j p e) -> r e p j", j=PACK, e=2),
+            )
+            free_bank(("dz1_bank", b, u))
+
+        def quantize_dz1_features(b, lo, hi):
+            if lo == 0:
+                tiles["dz1_d_mx", b] = mx_tiles(keep, "dz1_d_%d" % b, "dz1_d_%d" % b)
+            quantize(tiles["dz1_d_mx", b], E5M2, tiles["dz1_d", b][:, lo * W : hi * W], lo * P)
+
+        def multiply_p(b, t):
+            if b == 0:
+                take_bank(("p", 0, t))
+            product(tiles["p", 0, t], tiles["dz1_d_mx", b], E5M2, t, tiles["q_mx", b], E4M3, b == 0, b == SLABS - 1)
+
+        def row_sum(t):
+            nc.vector.scalar_tensor_tensor(
+                out=weighted[:].rearrange("p (m s) -> p m s", s=PACK),
+                in0=tiles["p", 0, t][:].rearrange("p (s m) -> p m s", s=PACK),
+                scalar=-1.0,
+                in1=nadj_sb[:, t, :].rearrange("p (m s) -> p m s", s=PACK),
+                op0=ALU.mult,
+                op1=ALU.mult,
+                accum_out=minus_sums[:, t : t + 1],
+            )
+
+        def finish_dadj(t):
+            result = keep.tile([P, W], F32, name="dadj_%d" % t)
+            nc.scalar.activation(
+                out=result[:].rearrange("p (m s) -> p m s", s=PACK),
+                in_=tiles["p", 0, t][:].rearrange("p (s m) -> p m s", s=PACK),
+                func=ACT.Identity,
+                bias=minus_sums[:, t : t + 1],
+            )
+            nc.sync.dma_start(out=dadj_hbm[:, t, :], in_=result[:])
+
+        identity = keep.tile([P, P], F32, name="identity")
+        make_identity(nc, identity[:])
+        weighted = keep.tile([P, W], F32, name="weighted")
+        minus_sums = keep.tile([P, PACK], F32, name="minus_sums")
+        wt_mx = mx_tiles(keep, "wt", "wt")
+        adj_mx = mx_tiles(keep, "adj", "adj")
+        wt_grouped = keep.tile([P, PACK * W], BF16, name="wt_grouped", align_bytes=64)
+        adj_grouped = keep.tile([P, PACK * W], BF16, name="adj_grouped", align_bytes=64)
+
+        load_rows("g", g_hbm, BF16, 0, 0, 2)
+        load_rows("z", z_hbm, F32, 0, 0, 1)
+        wt_sb = load("wt_sb", Wt.rearrange("(p s) d -> p s d", s=PACK), BF16)
+        load_rows("z", z_hbm, F32, 0, 1, 2)
+        load_rows("g", g_hbm, BF16, 0, 2, 4)
+        load_rows("z", z_hbm, F32, 0, 2, 3)
+        load_rows("z", z_hbm, F32, 0, 3, 4)
+        rdeg_sb = load("rdeg_sb", rdeg.rearrange("(p t) -> p t", t=PACK), F32)
+        load_grad(1, 0, 2)
+        load_grad(1, 2, 4)
+        adj_sb = load("adj_sb", adj.rearrange("(p s) m -> p s m", s=PACK), BF16)
+        load_grad(2, 0, 2)
+        load_query(0)
+        load_grad(2, 2, 4)
+        load_query(1)
+        load_grad(3, 0, 2)
+        load_query(2)
+        load_grad(3, 2, 4)
+        load_query(3)
+        nadj_sb = load("nadj_sb", nadj.rearrange("(p t) m -> p t m", t=PACK), F32)
+
+        wt_dst = wt_grouped[:].rearrange("p (c i s) -> p c s i", i=PACK, s=PACK)
+        wt_src = wt_sb[:].rearrange("p s (c i) -> p c s i", i=PACK)
+        adj_dst = adj_grouped[:].rearrange("p (t m s) -> p m s t", t=PACK, s=PACK)
+        adj_src = adj_sb[:].rearrange("p s (m t) -> p m s t", t=PACK)
+        take_bank(("warm", 0, 0))
+        warm(4)
+        mask(0, 0, 1)
+        turn_dz2(0, 0)
+        warm(3)
+        nc.scalar.activation(out=wt_dst[:, :40], in_=wt_src[:, :40], func=ACT.Copy)
+        nc.vector.tensor_copy(out=wt_dst[:, 40:], in_=wt_src[:, 40:])
+        copy_dz2(0, 0, 1)
+        mask(0, 1, 2)
+        turn_dz2(0, 1)
+        warm(2)
+        copy_dz2(0, 1, 2)
+        quantize(wt_mx, E4M3, wt_grouped[:], 0)
+        mask(0, 2, 3)
+        turn_dz2(0, 2)
+        copy_dz2(0, 2, 3)
+        quantize_dz2(0, 0)
+        multiply_dgq(0, 0)
+        mask(0, 3, 4)
+        quantize_dz2(0, 1)
+        turn_dz2(0, 3)
+        copy_dz2(0, 3, 4)
+        multiply_dgq(0, 1)
+        scale_dgq(0, 0)
+        quantize_dz2(0, 2)
+        multiply_dgq(0, 2)
+        mask(1, 0, 2)
+        quantize_dz2(0, 3)
+        multiply_dgq(0, 3)
+        scale_dgq(0, 1)
+        scale_dgq(0, 2)
+        scale_dgq(0, 3)
+        turn_dz2(1, 0)
+        warm(2)
+        free_bank(("warm", 0, 0))
+        copy_dz2(1, 0, 2)
+        mask(1, 2, 4)
+        turn_dz2(1, 2)
+        copy_dz2(1, 2, 4)
+        nc.vector.tensor_copy(out=adj_dst[:, ADJ_SHARE:], in_=adj_src[:, ADJ_SHARE:])
+        nc.scalar.copy(out=adj_dst[:, :ADJ_SHARE], in_=adj_src[:, :ADJ_SHARE])
+        quantize_dz2(1, 0)
+        multiply_dgq(1, 0, 2)
+        multiply_dgq(1, 1)
+
+        last = SLABS - 1
+        for b in range(last):
+            ahead2 = b + 2 < SLABS
+            if b > 0:
+                turn_query(b, 0)
+            round_dz1(b)
+            scale_dgq(b + 1, 0)
+            if b > 0:
+                copy_query(b, 0)
+            scale_dgq(b + 1, 1)
+            turn_dz1(b, 0)
+            quantize_dz2(b + 1, 2)
+            multiply_dgq(b + 1, 2)
+            multiply_dgq(b + 1, 3)
+            copy_dz1(b, 0)
+            quantize_dz1_nodes(b)
+            if b == 0:
+                quantize(adj_mx, E4M3, adj_grouped[:], 0)
+            multiply_dq(b, 0)
+            multiply_dq(b, 1)
+            if ahead2:
+                mask(b + 2, 0, 2)
+            if b > 0:
+                quantize_query(b - 1)
+            scale_dgq(b + 1, 2)
+            scale_dgq(b + 1, 3)
+            if not ahead2:
+                break
+            add_self_loop(b, 0)
+            add_self_loop(b, 1)
+            store_dq(b, 0, 2)
+            turn_dz2(b + 2, 0)
+            copy_dz2(b + 2, 0, 2)
+            turn_dz1(b, 1)
+            copy_dz1(b, 1)
+            multiply_dq(b, 2)
+            multiply_dq(b, 3)
+            if b == 0:
+                turn_query(0, 0)
+                copy_query(0, 0)
+            turn_query(b, 1)
+            copy_query(b, 1)
+            mask(b + 2, 2, 4)
+            add_self_loop(b, 2)
+            add_self_loop(b, 3)
+            store_dq(b, 2, 4)
+            turn_dz2(b + 2, 2)
+            copy_dz2(b + 2, 2, 4)
+            quantize_dz2(b + 2, 0)
+            quantize_dz1_features(b, 0, 4)
+            multiply_dgq(b + 2, 0, 2)
+            multiply_dgq(b + 2, 1)
+        turn_dz1(2, 1)
+        add_self_loop(2, 0)
+        add_self_loop(2, 1)
+        store_dq(2, 0, 2)
+        round_dz1(last)
+        copy_dz1(2, 1)
+        for early in range(2):
+            multiply_p(early, 0)
+        turn_query(2, 1)
+        copy_query(2, 1)
+        multiply_dq(2, 2)
+        multiply_dq(2, 3)
+        add_self_loop(2, 2)
+        turn_dz1(last, 0)
+        copy_dz1(last, 0)
+        quantize_dz1_nodes(last)
+        add_self_loop(2, 3)
+        store_dq(2, 2, 4)
+        for early in range(2):
+            multiply_p(early, 1)
+        turn_query(last, 0)
+        multiply_dq(last, 0)
+        multiply_dq(last, 1)
+        quantize_dz1_features(2, 0, 4)
+        quantize_query(2)
+        copy_query(last, 0)
+        turn_query(last, 1)
+        copy_query(last, 1)
+        for early in range(2):
+            multiply_p(early, 2)
+        turn_dz1(last, 1)
+        copy_dz1(last, 1)
+        add_self_loop(last, 0)
+        quantize_dz1_features(last, 0, 2)
+        add_self_loop(last, 1)
+        store_dq(last, 0, 2)
+        multiply_p(2, 0)
+        multiply_p(2, 1)
+        quantize_query(last)
+        multiply_dq(last, 2)
+        multiply_p(last, 0)
+        multiply_p(last, 1)
+        add_self_loop(last, 2)
+        store_dq(last, 2, 3)
+        for early in range(last):
+            multiply_p(early, 3)
+        multiply_p(2, 2)
+        quantize_dz1_features(last, 2, 4)
+        row_sum(0)
+        finish_dadj(0)
+        multiply_p(last, 2)
+        multiply_p(last, 3)
+        multiply_dq(last, 3)
+        for t in range(1, PACK):
+            row_sum(t)
+            finish_dadj(t)
+        add_self_loop(last, 3)
+        store_dq(last, 3, 4)

@@ -105,18 +105,19 @@ def tile_gatedspatialattentionlayer_pc_v_kernel(
         def mask(b, lo, hi):
             dz2 = stage.tile([P, (hi - lo) * W], BF16, name="dz2_%d_%d" % (b, lo), tag="dz2", bufs=4, align_bytes=64)
             tiles["dz2", b, lo] = dz2
-            nc.vector.scalar_tensor_tensor(
-                out=dz2[:],
-                in0=loaded_rows("z", b, lo, hi),
-                scalar=0.0,
-                in1=loaded_rows("g", b, lo, hi),
-                op0=ALU.is_gt,
-                op1=ALU.mult,
-            )
+            split = "p (w u e) -> p u w e"
+            for u in range(2):
+                nc.vector.scalar_tensor_tensor(
+                    out=dz2[:].rearrange("p (u w e) -> p u w e", u=2, e=2)[:, u],
+                    in0=loaded_rows("z", b, lo, hi).rearrange(split, u=2, e=2)[:, u],
+                    scalar=0.0,
+                    in1=loaded_rows("g", b, lo, hi).rearrange(split, u=2, e=2)[:, u],
+                    op0=ALU.is_gt,
+                    op1=ALU.mult,
+                )
 
-        def turn_rows(key, values):
+        def turn_rows(key, words):
             bank = take_bank(key)
-            words = values.bitcast(F32).rearrange("p (t w u) -> p t w u", w=P, u=2)
             for t in range(words.shape[1]):
                 for u in range(2):
                     at = (2 * t + u) * P
@@ -131,7 +132,8 @@ def tile_gatedspatialattentionlayer_pc_v_kernel(
             free_bank(key)
 
         def turn_dz2(b, lo):
-            turn_rows(("dz2_bank", b, lo), tiles["dz2", b, lo][:])
+            words = tiles["dz2", b, lo][:].bitcast(F32).rearrange("p (u t w) -> p t w u", u=2, w=P)
+            turn_rows(("dz2_bank", b, lo), words)
 
         def copy_dz2(b, lo, hi):
             turned = stage.tile([P, (hi - lo) * W], BF16, name="dz2_t_%d_%d" % (b, lo), tag="dz2_t", bufs=4, align_bytes=64)
@@ -144,7 +146,8 @@ def tile_gatedspatialattentionlayer_pc_v_kernel(
             quantize(tiles["dz2_mx", b], E5M2, tiles["dz2_t", b, lo][:], lo * P)
 
         def turn_query(b, h):
-            turn_rows(("q_bank", b, h), tiles["q", b][:].rearrange("p t d -> p (t d)")[:, h * 2 * W : (h + 1) * 2 * W])
+            words = tiles["q", b][:].bitcast(F32).rearrange("p t (w u) -> p t w u", u=2)
+            turn_rows(("q_bank", b, h), words[:, 2 * h : 2 * h + 2])
 
         def copy_query(b, h):
             if h == 0:
@@ -172,8 +175,8 @@ def tile_gatedspatialattentionlayer_pc_v_kernel(
         def round_dz1(b):
             rounded = stage.tile([P, PACK * W], BF16, name="dz1_n_%d" % b, tag="dz1_n", align_bytes=64)
             tiles["dz1_n", b] = rounded
-            dst = rounded[:].rearrange("p (j r t) -> p r t j", j=PACK, t=PACK)
-            src = tiles["dz1", b][:].rearrange("p t (r j) -> p r t j", j=PACK)
+            dst = rounded[:].rearrange("p (j r t) -> p r j t", j=PACK, t=PACK)
+            src = tiles["dz1", b][:].rearrange("p t (r j) -> p r j t", j=PACK)
             share = SCALAR_SHARE[b]
             if share:
                 nc.scalar.copy(out=dst[:, :share], in_=src[:, :share])
@@ -257,10 +260,9 @@ def tile_gatedspatialattentionlayer_pc_v_kernel(
         wt_grouped = keep.tile([P, PACK * W], BF16, name="wt_grouped", align_bytes=64)
         adj_grouped = keep.tile([P, PACK * W], BF16, name="adj_grouped", align_bytes=64)
 
-        load_rows("g", g_hbm, BF16, 0, 0, 2)
-        load_rows("z", z_hbm, F32, 0, 0, 1)
+        load_grad(0, 0, 1)
         wt_sb = load("wt_sb", Wt.rearrange("(p s) d -> p s d", s=PACK), BF16)
-        load_rows("z", z_hbm, F32, 0, 1, 2)
+        load_grad(0, 1, 2)
         load_rows("g", g_hbm, BF16, 0, 2, 4)
         load_rows("z", z_hbm, F32, 0, 2, 3)
         load_rows("z", z_hbm, F32, 0, 3, 4)
@@ -280,8 +282,8 @@ def tile_gatedspatialattentionlayer_pc_v_kernel(
 
         wt_dst = wt_grouped[:].rearrange("p (c i s) -> p c s i", i=PACK, s=PACK)
         wt_src = wt_sb[:].rearrange("p s (c i) -> p c s i", i=PACK)
-        adj_dst = adj_grouped[:].rearrange("p (t m s) -> p m s t", t=PACK, s=PACK)
-        adj_src = adj_sb[:].rearrange("p s (m t) -> p m s t", t=PACK)
+        adj_dst = adj_grouped[:].rearrange("p (t m s) -> p m t s", t=PACK, s=PACK)
+        adj_src = adj_sb[:].rearrange("p s (m t) -> p m t s", t=PACK)
         take_bank(("warm", 0, 0))
         warm(4)
         mask(0, 0, 1)
@@ -377,7 +379,10 @@ def tile_gatedspatialattentionlayer_pc_v_kernel(
             copy_dz2(b + 2, 2, 4)
             quantize_dz2(b + 2, 0)
             quantize_dz1_features(b, 0, 4)
-            multiply_dgq(b + 2, 0, 2)
+            if b > 0:
+                multiply_p(b - 1, 0)
+                multiply_p(b - 1, 1)
+            multiply_dgq(b + 2, 0, 0 if b else 2)
             multiply_dgq(b + 2, 1)
         turn_dz1(2, 1)
         add_self_loop(2, 0)
@@ -385,8 +390,8 @@ def tile_gatedspatialattentionlayer_pc_v_kernel(
         store_dq(2, 0, 2)
         round_dz1(last)
         copy_dz1(2, 1)
-        for early in range(2):
-            multiply_p(early, 0)
+        multiply_p(1, 0)
+        multiply_p(1, 1)
         turn_query(2, 1)
         copy_query(2, 1)
         multiply_dq(2, 2)
@@ -397,8 +402,6 @@ def tile_gatedspatialattentionlayer_pc_v_kernel(
         quantize_dz1_nodes(last)
         add_self_loop(2, 3)
         store_dq(2, 2, 4)
-        for early in range(2):
-            multiply_p(early, 1)
         turn_query(last, 0)
         multiply_dq(last, 0)
         multiply_dq(last, 1)
@@ -407,33 +410,33 @@ def tile_gatedspatialattentionlayer_pc_v_kernel(
         copy_query(last, 0)
         turn_query(last, 1)
         copy_query(last, 1)
-        for early in range(2):
-            multiply_p(early, 2)
         turn_dz1(last, 1)
         copy_dz1(last, 1)
         add_self_loop(last, 0)
         quantize_dz1_features(last, 0, 2)
         add_self_loop(last, 1)
         store_dq(last, 0, 2)
-        multiply_p(2, 0)
-        multiply_p(2, 1)
-        quantize_query(last)
+        for early in range(2):
+            multiply_p(early, 2)
         multiply_dq(last, 2)
+        for t in range(last):
+            multiply_p(2, t)
+        multiply_p(0, 3)
+        quantize_query(last)
         multiply_p(last, 0)
         multiply_p(last, 1)
         add_self_loop(last, 2)
         store_dq(last, 2, 3)
-        for early in range(last):
-            multiply_p(early, 3)
-        multiply_p(2, 2)
+        multiply_p(1, 3)
+        multiply_p(2, 3)
         quantize_dz1_features(last, 2, 4)
-        row_sum(0)
-        finish_dadj(0)
         multiply_p(last, 2)
         multiply_p(last, 3)
         multiply_dq(last, 3)
-        for t in range(1, PACK):
+        for t in range(last):
             row_sum(t)
             finish_dadj(t)
+        row_sum(last)
         add_self_loop(last, 3)
         store_dq(last, 3, 4)
+        finish_dadj(last)

@@ -18,7 +18,7 @@ W = 512
 SLABS = 4
 HALVES = 2
 BANKS = 8
-SCALAR_SHARE = [0, 24, 16, 32]
+SCALAR_SHARE = [0, 24, 32, 32]
 ADJ_SHARE = 64
 
 FLOPS = 3 * 2 * SLABS * W * W * W
@@ -103,18 +103,17 @@ def tile_gatedspatialattentionlayer_pc_v_kernel(
             tiles["q", b] = load("q_%d" % b, q_hbm[b], BF16)
 
         def mask(b, lo, hi):
-            dz2 = stage.tile([P, (hi - lo) * W], BF16, name="dz2_%d_%d" % (b, lo), tag="dz2", bufs=4, align_bytes=64)
-            tiles["dz2", b, lo] = dz2
-            split = "p (w u e) -> p u w e"
-            for u in range(2):
-                nc.vector.scalar_tensor_tensor(
-                    out=dz2[:].rearrange("p (u w e) -> p u w e", u=2, e=2)[:, u],
-                    in0=loaded_rows("z", b, lo, hi).rearrange(split, u=2, e=2)[:, u],
-                    scalar=0.0,
-                    in1=loaded_rows("g", b, lo, hi).rearrange(split, u=2, e=2)[:, u],
-                    op0=ALU.is_gt,
-                    op1=ALU.mult,
-                )
+            dz2 = stage.tile([P, (hi - lo) * W], BF16, name="dz2_%d_%d" % (b, lo), tag="dz2", bufs=3, align_bytes=64)
+            for t in range(lo, hi):
+                tiles["dz2", b, t] = (dz2, lo)
+            nc.vector.scalar_tensor_tensor(
+                out=dz2[:],
+                in0=loaded_rows("z", b, lo, hi),
+                scalar=0.0,
+                in1=loaded_rows("g", b, lo, hi),
+                op0=ALU.is_gt,
+                op1=ALU.mult,
+            )
 
         def turn_rows(key, words):
             bank = take_bank(key)
@@ -123,36 +122,37 @@ def tile_gatedspatialattentionlayer_pc_v_kernel(
                     at = (2 * t + u) * P
                     nc.tensor.transpose(bank[:, at : at + P], words[:, t, :, u], identity[:])
 
-        def copy_rows(key, turned):
+        def copy_rows(key, turned, move=nc.scalar.copy):
             width = turned.shape[1] // 2
-            nc.scalar.copy(
+            move(
                 out=turned.bitcast(F32).rearrange("w (t p u) -> w t p u", p=P, u=2),
                 in_=tiles[key][:, :width].rearrange("w (t u p) -> w t p u", p=P, u=2),
             )
             free_bank(key)
 
-        def turn_dz2(b, lo):
-            words = tiles["dz2", b, lo][:].bitcast(F32).rearrange("p (u t w) -> p t w u", u=2, w=P)
-            turn_rows(("dz2_bank", b, lo), words)
+        def turn_dz2(b, lo, hi):
+            dz2, first = tiles["dz2", b, lo]
+            words = dz2[:].bitcast(F32).rearrange("p (t w u) -> p t w u", u=2, w=P)
+            turn_rows(("dz2_bank", b, lo), words[:, lo - first : hi - first])
 
         def copy_dz2(b, lo, hi):
-            turned = stage.tile([P, (hi - lo) * W], BF16, name="dz2_t_%d_%d" % (b, lo), tag="dz2_t", bufs=4, align_bytes=64)
-            tiles["dz2_t", b, lo] = turned
-            copy_rows(("dz2_bank", b, lo), turned[:])
+            if lo == 0:
+                tiles["dz2_t", b] = stage.tile([P, PACK * W], BF16, name="dz2_t_%d" % b, tag="dz2_t", align_bytes=64)
+            copy_rows(("dz2_bank", b, lo), tiles["dz2_t", b][:, lo * W : hi * W])
 
-        def quantize_dz2(b, lo):
+        def quantize_dz2(b, lo, hi):
             if lo == 0:
                 tiles["dz2_mx", b] = mx_tiles(stage, "dz2_%d" % b, "dz2")
-            quantize(tiles["dz2_mx", b], E5M2, tiles["dz2_t", b, lo][:], lo * P)
+            quantize(tiles["dz2_mx", b], E5M2, tiles["dz2_t", b][:, lo * W : hi * W], lo * P)
 
         def turn_query(b, h):
             words = tiles["q", b][:].bitcast(F32).rearrange("p t (w u) -> p t w u", u=2)
             turn_rows(("q_bank", b, h), words[:, 2 * h : 2 * h + 2])
 
-        def copy_query(b, h):
+        def copy_query(b, h, move=nc.scalar.copy):
             if h == 0:
                 tiles["q_t", b] = stage.tile([P, PACK * W], BF16, name="q_t_%d" % b, tag="q_t", bufs=3, align_bytes=64)
-            copy_rows(("q_bank", b, h), tiles["q_t", b][:, h * 2 * W : (h + 1) * 2 * W])
+            copy_rows(("q_bank", b, h), tiles["q_t", b][:, h * 2 * W : (h + 1) * 2 * W], move)
 
         def quantize_query(b):
             tiles["q_mx", b] = mx_tiles(keep, "q_%d" % b, "q_%d" % b)
@@ -174,7 +174,7 @@ def tile_gatedspatialattentionlayer_pc_v_kernel(
 
         def round_dz1(b):
             rounded = stage.tile([P, PACK * W], BF16, name="dz1_n_%d" % b, tag="dz1_n", align_bytes=64)
-            tiles["dz1_n", b] = rounded
+            tiles["dz1_n", b] = rounded[:]
             dst = rounded[:].rearrange("p (j r t) -> p r j t", j=PACK, t=PACK)
             src = tiles["dz1", b][:].rearrange("p t (r j) -> p r j t", j=PACK)
             share = SCALAR_SHARE[b]
@@ -184,7 +184,7 @@ def tile_gatedspatialattentionlayer_pc_v_kernel(
 
         def quantize_dz1_nodes(b):
             tiles["dz1_n_mx", b] = mx_tiles(stage, "dz1_n_%d" % b, "dz1_n")
-            quantize(tiles["dz1_n_mx", b], E5M2, tiles["dz1_n", b][:], 0)
+            quantize(tiles["dz1_n_mx", b], E5M2, tiles["dz1_n", b], 0)
 
         def multiply_dq(b, t):
             product(take_bank(("dq", b, t)), adj_mx, E4M3, t, tiles["dz1_n_mx", b], E5M2, True, True)
@@ -207,7 +207,7 @@ def tile_gatedspatialattentionlayer_pc_v_kernel(
             bank = take_bank(("dz1_bank", b, u))
             for n in range(warmers):
                 nc.tensor.matmul(bank[:, :P], lhsT=identity[:], rhs=identity[:], start=True, stop=True)
-            words = tiles["dz1_n", b][:].bitcast(F32).rearrange("p (j r u) -> p j r u", j=PACK, u=2)
+            words = tiles["dz1_n", b].bitcast(F32).rearrange("p (j r u) -> p j r u", j=PACK, u=2)
             for j in range(PACK):
                 nc.tensor.transpose(bank[:, j * P : (j + 1) * P], words[:, j, :, u], identity[:])
 
@@ -241,15 +241,18 @@ def tile_gatedspatialattentionlayer_pc_v_kernel(
                 accum_out=minus_sums[:, t : t + 1],
             )
 
-        def finish_dadj(t):
-            result = keep.tile([P, W], F32, name="dadj_%d" % t)
-            nc.scalar.activation(
-                out=result[:].rearrange("p (m s) -> p m s", s=PACK),
-                in_=tiles["p", 0, t][:].rearrange("p (s m) -> p m s", s=PACK),
-                func=ACT.Identity,
-                bias=minus_sums[:, t : t + 1],
-            )
-            nc.sync.dma_start(out=dadj_hbm[:, t, :], in_=result[:])
+        def finish_dadj(t, parts=1):
+            width = W // parts
+            for part in range(parts):
+                cols = slice(part * width, (part + 1) * width)
+                result = keep.tile([P, width], F32, name="dadj_%d_%d" % (t, part))
+                nc.scalar.activation(
+                    out=result[:].rearrange("p (m s) -> p m s", s=PACK),
+                    in_=tiles["p", 0, t][:].rearrange("p (s m) -> p m s", s=PACK)[:, cols.start // PACK : cols.stop // PACK],
+                    func=ACT.Identity,
+                    bias=minus_sums[:, t : t + 1],
+                )
+                nc.sync.dma_start(out=dadj_hbm[:, t, cols], in_=result[:])
 
         identity = keep.tile([P, P], F32, name="identity")
         make_identity(nc, identity[:])
@@ -287,51 +290,50 @@ def tile_gatedspatialattentionlayer_pc_v_kernel(
         take_bank(("warm", 0, 0))
         warm(4)
         mask(0, 0, 1)
-        turn_dz2(0, 0)
+        turn_dz2(0, 0, 1)
         warm(3)
         nc.scalar.activation(out=wt_dst[:, :40], in_=wt_src[:, :40], func=ACT.Copy)
         nc.vector.tensor_copy(out=wt_dst[:, 40:], in_=wt_src[:, 40:])
         copy_dz2(0, 0, 1)
         mask(0, 1, 2)
-        turn_dz2(0, 1)
+        turn_dz2(0, 1, 2)
         warm(2)
         copy_dz2(0, 1, 2)
         quantize(wt_mx, E4M3, wt_grouped[:], 0)
         mask(0, 2, 3)
-        turn_dz2(0, 2)
+        turn_dz2(0, 2, 3)
         copy_dz2(0, 2, 3)
-        quantize_dz2(0, 0)
+        quantize_dz2(0, 0, 1)
         multiply_dgq(0, 0)
         mask(0, 3, 4)
-        quantize_dz2(0, 1)
-        turn_dz2(0, 3)
+        quantize_dz2(0, 1, 2)
+        turn_dz2(0, 3, 4)
         copy_dz2(0, 3, 4)
         multiply_dgq(0, 1)
         scale_dgq(0, 0)
-        quantize_dz2(0, 2)
+        quantize_dz2(0, 2, 3)
         multiply_dgq(0, 2)
+        warm(2)
         mask(1, 0, 2)
-        quantize_dz2(0, 3)
+        quantize_dz2(0, 3, 4)
         multiply_dgq(0, 3)
         scale_dgq(0, 1)
         scale_dgq(0, 2)
         scale_dgq(0, 3)
-        turn_dz2(1, 0)
-        warm(2)
+        turn_dz2(1, 0, 2)
         free_bank(("warm", 0, 0))
         copy_dz2(1, 0, 2)
         mask(1, 2, 4)
-        turn_dz2(1, 2)
+        turn_dz2(1, 2, 4)
         copy_dz2(1, 2, 4)
         nc.vector.tensor_copy(out=adj_dst[:, ADJ_SHARE:], in_=adj_src[:, ADJ_SHARE:])
         nc.scalar.copy(out=adj_dst[:, :ADJ_SHARE], in_=adj_src[:, :ADJ_SHARE])
-        quantize_dz2(1, 0)
+        quantize_dz2(1, 0, 2)
         multiply_dgq(1, 0, 2)
         multiply_dgq(1, 1)
 
         last = SLABS - 1
-        for b in range(last):
-            ahead2 = b + 2 < SLABS
+        for b in range(last - 1):
             if b > 0:
                 turn_query(b, 0)
             round_dz1(b)
@@ -340,7 +342,7 @@ def tile_gatedspatialattentionlayer_pc_v_kernel(
                 copy_query(b, 0)
             scale_dgq(b + 1, 1)
             turn_dz1(b, 0)
-            quantize_dz2(b + 1, 2)
+            quantize_dz2(b + 1, 2, 4)
             multiply_dgq(b + 1, 2)
             multiply_dgq(b + 1, 3)
             copy_dz1(b, 0)
@@ -349,18 +351,15 @@ def tile_gatedspatialattentionlayer_pc_v_kernel(
                 quantize(adj_mx, E4M3, adj_grouped[:], 0)
             multiply_dq(b, 0)
             multiply_dq(b, 1)
-            if ahead2:
-                mask(b + 2, 0, 2)
+            mask(b + 2, 0, 2)
             if b > 0:
                 quantize_query(b - 1)
             scale_dgq(b + 1, 2)
             scale_dgq(b + 1, 3)
-            if not ahead2:
-                break
             add_self_loop(b, 0)
             add_self_loop(b, 1)
             store_dq(b, 0, 2)
-            turn_dz2(b + 2, 0)
+            turn_dz2(b + 2, 0, 2)
             copy_dz2(b + 2, 0, 2)
             turn_dz1(b, 1)
             copy_dz1(b, 1)
@@ -375,54 +374,70 @@ def tile_gatedspatialattentionlayer_pc_v_kernel(
             add_self_loop(b, 2)
             add_self_loop(b, 3)
             store_dq(b, 2, 4)
-            turn_dz2(b + 2, 2)
+            turn_dz2(b + 2, 2, 4)
             copy_dz2(b + 2, 2, 4)
-            quantize_dz2(b + 2, 0)
+            quantize_dz2(b + 2, 0, 2)
             quantize_dz1_features(b, 0, 4)
             if b > 0:
                 multiply_p(b - 1, 0)
                 multiply_p(b - 1, 1)
             multiply_dgq(b + 2, 0, 0 if b else 2)
             multiply_dgq(b + 2, 1)
-        turn_dz1(2, 1)
+        turn_query(2, 0)
+        round_dz1(2)
+        scale_dgq(last, 0)
+        scale_dgq(last, 1)
+        quantize_dz2(last, 2, 4)
+        multiply_dgq(last, 2)
+        multiply_dgq(last, 3)
+        quantize_dz1_nodes(2)
+        multiply_dq(2, 0)
+        multiply_dq(2, 1)
+        copy_query(2, 0)
+        scale_dgq(last, 2)
+        scale_dgq(last, 3)
+        quantize_query(1)
+        turn_dz1(2, 0)
         add_self_loop(2, 0)
         add_self_loop(2, 1)
         store_dq(2, 0, 2)
         round_dz1(last)
+        copy_dz1(2, 0)
+        multiply_dq(2, 2)
+        multiply_dq(2, 3)
+        turn_dz1(2, 1)
         copy_dz1(2, 1)
+        add_self_loop(2, 2)
         multiply_p(1, 0)
         multiply_p(1, 1)
         turn_query(2, 1)
         copy_query(2, 1)
-        multiply_dq(2, 2)
-        multiply_dq(2, 3)
-        add_self_loop(2, 2)
-        turn_dz1(last, 0)
-        copy_dz1(last, 0)
         quantize_dz1_nodes(last)
         add_self_loop(2, 3)
         store_dq(2, 2, 4)
-        turn_query(last, 0)
+        turn_dz1(last, 0)
+        copy_dz1(last, 0)
         multiply_dq(last, 0)
         multiply_dq(last, 1)
+        turn_query(last, 0)
         quantize_dz1_features(2, 0, 4)
+        add_self_loop(last, 0)
         quantize_query(2)
-        copy_query(last, 0)
+        copy_query(last, 0, nc.vector.tensor_copy)
         turn_query(last, 1)
         copy_query(last, 1)
         turn_dz1(last, 1)
         copy_dz1(last, 1)
-        add_self_loop(last, 0)
-        quantize_dz1_features(last, 0, 2)
         add_self_loop(last, 1)
         store_dq(last, 0, 2)
         for early in range(2):
             multiply_p(early, 2)
         multiply_dq(last, 2)
+        quantize_dz1_features(last, 0, 2)
         for t in range(last):
             multiply_p(2, t)
-        multiply_p(0, 3)
         quantize_query(last)
+        multiply_p(0, 3)
         multiply_p(last, 0)
         multiply_p(last, 1)
         add_self_loop(last, 2)

from contextlib import ExitStack

import concourse.mybir as mybir
from concourse.masks import make_identity

F32 = mybir.dt.float32
BF16 = mybir.dt.bfloat16
U32 = mybir.dt.uint32
U8 = mybir.dt.uint8
E4M3 = mybir.dt.float8_e4m3fn_x4
E5M2 = mybir.dt.float8_e5m2_x4
ALU = mybir.AluOpType
ACT = mybir.ActivationFunctionType

P = 128
PACK = 4
W = 512
SLABS = 4
HALVES = 2
BANKS = 8
SCALAR_SHARE = [0, 24, 32, 32]
ADJ_SHARE = 64

FLOPS = 3 * 2 * SLABS * W * W * W
BYTES = 2 * (2 * W * W + 2 * SLABS * W * W) + 4 * (SLABS * W * W + W * W + W) + 4 * (SLABS * W * W + W * W)


def tile_gatedspatialattentionlayer_pc_v_kernel(
    tc, adj, query, Wt, bt, z2, nadj, rdeg, grad_out, out_0, out_1
):
    nc = tc.nc
    rows = "b s (p t) w -> (b s) p t w"
    z_hbm = z2.rearrange(rows, t=PACK)
    g_hbm = grad_out.rearrange(rows, t=PACK)
    q_hbm = query.rearrange(rows, t=PACK)
    o_hbm = out_0.rearrange(rows, t=PACK)
    dadj_hbm = out_1.rearrange("(p t) m -> p t m", t=PACK)

    with ExitStack() as ctx:
        keep = ctx.enter_context(tc.tile_pool(name="keep", bufs=1))
        stage = ctx.enter_context(tc.tile_pool(name="stage", bufs=2))
        psum = ctx.enter_context(tc.psum_pool(name="psum", bufs=1))
        ctx.enter_context(tc.manual_schedule())

        tiles = {}
        free_banks = list(range(BANKS))
        bank_of = {}

        def take_bank(key):
            number = free_banks.pop(0)
            bank_of[key] = number
            tiles[key] = psum.tile([P, W], F32, name="%s_%d_%d" % key, tag="bank%d" % number)
            return tiles[key]

        def free_bank(key):
            free_banks.append(bank_of[key])

        def mx_tiles(pool, name, tag):
            codes = pool.tile([P, W], U32, name=name + "_codes", tag=tag + "_codes", align_bytes=64)
            scales = pool.tile([P, W], U8, name=name + "_scales", tag=tag + "_scales", align_bytes=64)
            return codes, scales

        def quantize(operand, fmt, values, first):
            codes, scales = operand
            cols = slice(first, first + values.shape[1] // PACK)
            nc.vector.quantize_mx(out=codes[:, cols].bitcast(fmt), scales=scales[:, cols], in_=values)

        def product(out, stationary, stationary_fmt, t, moving, moving_fmt, start, stop):
            cols = slice(t * P, (t + 1) * P)
            nc.tensor.matmul_mx(
                out=out[:],
                lhsT=stationary[0][:, cols].bitcast(stationary_fmt),
                lhsT_scale=stationary[1][:, cols],
                rhs=moving[0][:].bitcast(moving_fmt),
                rhs_scale=moving[1][:],
                start=start,
                stop=stop,
            )

        def load(name, source, dtype):
            tile = keep.tile(list(source.shape), dtype, name=name, align_bytes=64)
            nc.sync.dma_start(out=tile[:], in_=source)
            return tile

        def load_rows(name, hbm, dtype, b, lo, hi):
            tile = load("%s_%d_%d" % (name, b, lo), hbm[b][:, lo:hi, :], dtype)
            for t in range(lo, hi):
                tiles[name, b, t] = (tile, lo)

        def loaded_rows(name, b, lo, hi):
            tile, first = tiles[name, b, lo]
            return tile[:, lo - first : hi - first, :].rearrange("p t o -> p (t o)")

        def load_grad(b, lo, hi):
            load_rows("g", g_hbm, BF16, b, lo, hi)
            load_rows("z", z_hbm, F32, b, lo, hi)

        def warm(count):
            for n in range(count):
                nc.tensor.matmul(tiles["warm", 0, 0][:, :P], lhsT=identity[:], rhs=identity[:], start=True, stop=True)

        def load_query(b):
            tiles["q", b] = load("q_%d" % b, q_hbm[b], BF16)

        def mask(b, lo, hi):
            dz2 = stage.tile([P, (hi - lo) * W], BF16, name="dz2_%d_%d" % (b, lo), tag="dz2", bufs=3, align_bytes=64)
            for t in range(lo, hi):
                tiles["dz2", b, t] = (dz2, lo)
            nc.vector.scalar_tensor_tensor(
                out=dz2[:],
                in0=loaded_rows("z", b, lo, hi),
                scalar=0.0,
                in1=loaded_rows("g", b, lo, hi),
                op0=ALU.is_gt,
                op1=ALU.mult,
            )

        def turn_rows(key, words):
            bank = take_bank(key)
            for t in range(words.shape[1]):
                for u in range(2):
                    at = (2 * t + u) * P
                    nc.tensor.transpose(bank[:, at : at + P], words[:, t, :, u], identity[:])

        def copy_rows(key, turned, move=nc.scalar.copy):
            width = turned.shape[1] // 2
            move(
                out=turned.bitcast(F32).rearrange("w (t p u) -> w t p u", p=P, u=2),
                in_=tiles[key][:, :width].rearrange("w (t u p) -> w t p u", p=P, u=2),
            )
            free_bank(key)

        def turn_dz2(b, lo, hi):
            dz2, first = tiles["dz2", b, lo]
            words = dz2[:].bitcast(F32).rearrange("p (t w u) -> p t w u", u=2, w=P)
            turn_rows(("dz2_bank", b, lo), words[:, lo - first : hi - first])

        def copy_dz2(b, lo, hi):
            if lo == 0:
                tiles["dz2_t", b] = stage.tile([P, PACK * W], BF16, name="dz2_t_%d" % b, tag="dz2_t", align_bytes=64)
            copy_rows(("dz2_bank", b, lo), tiles["dz2_t", b][:, lo * W : hi * W])

        def quantize_dz2(b, lo, hi):
            if lo == 0:
                tiles["dz2_mx", b] = mx_tiles(stage, "dz2_%d" % b, "dz2")
            quantize(tiles["dz2_mx", b], E5M2, tiles["dz2_t", b][:, lo * W : hi * W], lo * P)

        def turn_query(b, h):
            words = tiles["q", b][:].bitcast(F32).rearrange("p t (w u) -> p t w u", u=2)
            turn_rows(("q_bank", b, h), words[:, 2 * h : 2 * h + 2])

        def copy_query(b, h, move=nc.scalar.copy):
            if h == 0:
                tiles["q_t", b] = stage.tile([P, PACK * W], BF16, name="q_t_%d" % b, tag="q_t", bufs=3, align_bytes=64)
            copy_rows(("q_bank", b, h), tiles["q_t", b][:, h * 2 * W : (h + 1) * 2 * W], move)

        def quantize_query(b):
            tiles["q_mx", b] = mx_tiles(keep, "q_%d" % b, "q_%d" % b)
            quantize(tiles["q_mx", b], E4M3, tiles["q_t", b][:], 0)

        def multiply_dgq(b, t, warmers=0):
            bank = take_bank(("dgq", b, t))
            for n in range(warmers):
                nc.tensor.matmul(bank[:, :P], lhsT=identity[:], rhs=identity[:], start=True, stop=True)
            product(bank, tiles["dz2_mx", b], E5M2, t, wt_mx, E4M3, True, True)

        def scale_dgq(b, t):
            if t == 0:
                tiles["dz1", b] = stage.tile([P, PACK, W], F32, name="dz1_%d" % b, tag="dz1", bufs=3, align_bytes=64)
            nc.scalar.activation(
                out=tiles["dz1", b][:, t, :], in_=tiles["dgq", b, t][:], func=ACT.Copy, scale=rdeg_sb[:, t : t + 1]
            )
            free_bank(("dgq", b, t))

        def round_dz1(b):
            rounded = stage.tile([P, PACK * W], BF16, name="dz1_n_%d" % b, tag="dz1_n", align_bytes=64)
            tiles["dz1_n", b] = rounded[:]
            dst = rounded[:].rearrange("p (j r t) -> p r j t", j=PACK, t=PACK)
            src = tiles["dz1", b][:].rearrange("p t (r j) -> p r j t", j=PACK)
            share = SCALAR_SHARE[b]
            if share:
                nc.scalar.copy(out=dst[:, :share], in_=src[:, :share])
            nc.vector.tensor_copy(out=dst[:, share:], in_=src[:, share:])

        def quantize_dz1_nodes(b):
            tiles["dz1_n_mx", b] = mx_tiles(stage, "dz1_n_%d" % b, "dz1_n")
            quantize(tiles["dz1_n_mx", b], E5M2, tiles["dz1_n", b], 0)

        def multiply_dq(b, t):
            product(take_bank(("dq", b, t)), adj_mx, E4M3, t, tiles["dz1_n_mx", b], E5M2, True, True)

        def add_self_loop(b, t):
            if t == 0:
                tiles["o", b] = stage.tile([P, PACK, W], F32, name="o_%d" % b, tag="o", bufs=3)
            nc.vector.tensor_tensor(
                out=tiles["o", b][:, t, :].rearrange("p (r j) -> p r j", j=PACK),
                in0=tiles["dq", b, t][:].rearrange("p (j r) -> p r j", j=PACK),
                in1=tiles["dz1", b][:, t, :].rearrange("p (r j) -> p r j", j=PACK),
                op=ALU.add,
            )
            free_bank(("dq", b, t))

        def store_dq(b, lo, hi):
            nc.sync.dma_start(out=o_hbm[b][:, lo:hi, :], in_=tiles["o", b][:, lo:hi, :])

        def turn_dz1(b, u, warmers=0):
            bank = take_bank(("dz1_bank", b, u))
            for n in range(warmers):
                nc.tensor.matmul(bank[:, :P], lhsT=identity[:], rhs=identity[:], start=True, stop=True)
            words = tiles["dz1_n", b].bitcast(F32).rearrange("p (j r u) -> p j r u", j=PACK, u=2)
            for j in range(PACK):
                nc.tensor.transpose(bank[:, j * P : (j + 1) * P], words[:, j, :, u], identity[:])

        def copy_dz1(b, u):
            if u == 0:
                tiles["dz1_d", b] = stage.tile([P, PACK * W], BF16, name="dz1_d_%d" % b, tag="dz1_d", align_bytes=64)
            nc.scalar.copy(
                out=tiles["dz1_d", b][:, u * 2 * W : (u + 1) * 2 * W].rearrange("r (e p j) -> r e p j", e=2, j=PACK),
                in_=tiles["dz1_bank", b, u][:].bitcast(BF16).rearrange("r (j p e) -> r e p j", j=PACK, e=2),
            )
            free_bank(("dz1_bank", b, u))

        def quantize_dz1_features(b, lo, hi):
            if lo == 0:
                tiles["dz1_d_mx", b] = mx_tiles(keep, "dz1_d_%d" % b, "dz1_d_%d" % b)
            quantize(tiles["dz1_d_mx", b], E5M2, tiles["dz1_d", b][:, lo * W : hi * W], lo * P)

        def multiply_p(b, t):
            if b == 0:
                take_bank(("p", 0, t))
            product(tiles["p", 0, t], tiles["dz1_d_mx", b], E5M2, t, tiles["q_mx", b], E4M3, b == 0, b == SLABS - 1)

        def row_sum(t):
            nc.vector.scalar_tensor_tensor(
                out=weighted[:].rearrange("p (m s) -> p m s", s=PACK),
                in0=tiles["p", 0, t][:].rearrange("p (s m) -> p m s", s=PACK),
                scalar=-1.0,
                in1=nadj_sb[:, t, :].rearrange("p (m s) -> p m s", s=PACK),
                op0=ALU.mult,
                op1=ALU.mult,
                accum_out=minus_sums[:, t : t + 1],
            )

        def finish_dadj(t, parts=1):
            width = W // parts
            for part in range(parts):
                cols = slice(part * width, (part + 1) * width)
                result = keep.tile([P, width], F32, name="dadj_%d_%d" % (t, part))
                nc.scalar.activation(
                    out=result[:].rearrange("p (m s) -> p m s", s=PACK),
                    in_=tiles["p", 0, t][:].rearrange("p (s m) -> p m s", s=PACK)[:, cols.start // PACK : cols.stop // PACK],
                    func=ACT.Identity,
                    bias=minus_sums[:, t : t + 1],
                )
                nc.sync.dma_start(out=dadj_hbm[:, t, cols], in_=result[:])

        identity = keep.tile([P, P], F32, name="identity")
        make_identity(nc, identity[:])
        weighted = keep.tile([P, W], F32, name="weighted")
        minus_sums = keep.tile([P, PACK], F32, name="minus_sums")
        wt_mx = mx_tiles(keep, "wt", "wt")
        adj_mx = mx_tiles(keep, "adj", "adj")
        wt_grouped = keep.tile([P, PACK * W], BF16, name="wt_grouped", align_bytes=64)
        adj_grouped = keep.tile([P, PACK * W], BF16, name="adj_grouped", align_bytes=64)

        load_grad(0, 0, 1)
        wt_sb = load("wt_sb", Wt.rearrange("(p s) d -> p s d", s=PACK), BF16)
        load_grad(0, 1, 2)
        load_rows("g", g_hbm, BF16, 0, 2, 4)
        load_rows("z", z_hbm, F32, 0, 2, 3)
        load_rows("z", z_hbm, F32, 0, 3, 4)
        rdeg_sb = load("rdeg_sb", rdeg.rearrange("(p t) -> p t", t=PACK), F32)
        load_grad(1, 0, 2)
        load_grad(1, 2, 4)
        adj_sb = load("adj_sb", adj.rearrange("(p s) m -> p s m", s=PACK), BF16)
        load_grad(2, 0, 2)
        load_query(0)
        load_grad(2, 2, 4)
        load_query(1)
        load_grad(3, 0, 2)
        load_query(2)
        load_grad(3, 2, 4)
        load_query(3)
        nadj_sb = load("nadj_sb", nadj.rearrange("(p t) m -> p t m", t=PACK), F32)

        wt_dst = wt_grouped[:].rearrange("p (c i s) -> p c s i", i=PACK, s=PACK)
        wt_src = wt_sb[:].rearrange("p s (c i) -> p c s i", i=PACK)
        adj_dst = adj_grouped[:].rearrange("p (t m s) -> p m t s", t=PACK, s=PACK)
        adj_src = adj_sb[:].rearrange("p s (m t) -> p m t s", t=PACK)
        take_bank(("warm", 0, 0))
        warm(4)
        mask(0, 0, 1)
        turn_dz2(0, 0, 1)
        warm(3)
        nc.scalar.activation(out=wt_dst[:, :40], in_=wt_src[:, :40], func=ACT.Copy)
        nc.vector.tensor_copy(out=wt_dst[:, 40:], in_=wt_src[:, 40:])
        copy_dz2(0, 0, 1)
        mask(0, 1, 2)
        turn_dz2(0, 1, 2)
        warm(2)
        copy_dz2(0, 1, 2)
        quantize(wt_mx, E4M3, wt_grouped[:], 0)
        mask(0, 2, 3)
        turn_dz2(0, 2, 3)
        copy_dz2(0, 2, 3)
        quantize_dz2(0, 0, 1)
        multiply_dgq(0, 0)
        mask(0, 3, 4)
        quantize_dz2(0, 1, 2)
        turn_dz2(0, 3, 4)
        copy_dz2(0, 3, 4)
        multiply_dgq(0, 1)
        scale_dgq(0, 0)
        quantize_dz2(0, 2, 3)
        multiply_dgq(0, 2)
        warm(2)
        mask(1, 0, 2)
        quantize_dz2(0, 3, 4)
        multiply_dgq(0, 3)
        scale_dgq(0, 1)
        scale_dgq(0, 2)
        scale_dgq(0, 3)
        turn_dz2(1, 0, 2)
        free_bank(("warm", 0, 0))
        copy_dz2(1, 0, 2)
        mask(1, 2, 4)
        turn_dz2(1, 2, 4)
        copy_dz2(1, 2, 4)
        nc.vector.tensor_copy(out=adj_dst[:, ADJ_SHARE:], in_=adj_src[:, ADJ_SHARE:])
        nc.scalar.copy(out=adj_dst[:, :ADJ_SHARE], in_=adj_src[:, :ADJ_SHARE])
        quantize_dz2(1, 0, 2)
        multiply_dgq(1, 0, 2)
        multiply_dgq(1, 1)

        last = SLABS - 1
        for b in range(last - 1):
            if b > 0:
                turn_query(b, 0)
            round_dz1(b)
            scale_dgq(b + 1, 0)
            if b > 0:
                copy_query(b, 0)
            scale_dgq(b + 1, 1)
            turn_dz1(b, 0)
            quantize_dz2(b + 1, 2, 4)
            multiply_dgq(b + 1, 2)
            multiply_dgq(b + 1, 3)
            copy_dz1(b, 0)
            quantize_dz1_nodes(b)
            if b == 0:
                quantize(adj_mx, E4M3, adj_grouped[:], 0)
            multiply_dq(b, 0)
            multiply_dq(b, 1)
            mask(b + 2, 0, 2)
            if b > 0:
                quantize_query(b - 1)
            scale_dgq(b + 1, 2)
            scale_dgq(b + 1, 3)
            add_self_loop(b, 0)
            add_self_loop(b, 1)
            store_dq(b, 0, 2)
            turn_dz2(b + 2, 0, 2)
            copy_dz2(b + 2, 0, 2)
            turn_dz1(b, 1)
            copy_dz1(b, 1)
            multiply_dq(b, 2)
            multiply_dq(b, 3)
            if b == 0:
                turn_query(0, 0)
                copy_query(0, 0)
            turn_query(b, 1)
            copy_query(b, 1)
            mask(b + 2, 2, 4)
            add_self_loop(b, 2)
            add_self_loop(b, 3)
            store_dq(b, 2, 4)
            turn_dz2(b + 2, 2, 4)
            copy_dz2(b + 2, 2, 4)
            quantize_dz2(b + 2, 0, 2)
            quantize_dz1_features(b, 0, 4)
            if b > 0:
                multiply_p(b - 1, 0)
                multiply_p(b - 1, 1)
            multiply_dgq(b + 2, 0, 0 if b else 2)
            multiply_dgq(b + 2, 1)
        turn_query(2, 0)
        round_dz1(2)
        scale_dgq(last, 0)
        scale_dgq(last, 1)
        quantize_dz2(last, 2, 4)
        multiply_dgq(last, 2)
        multiply_dgq(last, 3)
        quantize_dz1_nodes(2)
        multiply_dq(2, 0)
        multiply_dq(2, 1)
        copy_query(2, 0)
        scale_dgq(last, 2)
        scale_dgq(last, 3)
        quantize_query(1)
        turn_dz1(2, 0)
        add_self_loop(2, 0)
        add_self_loop(2, 1)
        store_dq(2, 0, 2)
        round_dz1(last)
        copy_dz1(2, 0)
        multiply_dq(2, 2)
        multiply_dq(2, 3)
        turn_dz1(2, 1)
        copy_dz1(2, 1)
        add_self_loop(2, 2)
        multiply_p(1, 0)
        multiply_p(1, 1)
        turn_query(2, 1)
        copy_query(2, 1)
        quantize_dz1_nodes(last)
        add_self_loop(2, 3)
        store_dq(2, 2, 4)
        turn_dz1(last, 0)
        copy_dz1(last, 0)
        multiply_dq(last, 0)
        multiply_dq(last, 1)
        turn_query(last, 0)
        quantize_dz1_features(2, 0, 4)
        add_self_loop(last, 0)
        quantize_query(2)
        copy_query(last, 0, nc.vector.tensor_copy)
        turn_query(last, 1)
        copy_query(last, 1)
        turn_dz1(last, 1)
        copy_dz1(last, 1)
        add_self_loop(last, 1)
        store_dq(last, 0, 2)
        for early in range(2):
            multiply_p(early, 2)
        multiply_dq(last, 2)
        quantize_dz1_features(last, 0, 2)
        for t in range(last):
            multiply_p(2, t)
        quantize_query(last)
        multiply_p(0, 3)
        multiply_p(last, 0)
        multiply_p(last, 1)
        add_self_loop(last, 2)
        store_dq(last, 2, 3)
        multiply_p(1, 3)
        multiply_p(2, 3)
        quantize_dz1_features(last, 2, 4)
        multiply_p(last, 2)
        multiply_p(last, 3)
        multiply_dq(last, 3)
        for t in range(last):
            row_sum(t)
            finish_dadj(t)
        row_sum(last)
        add_self_loop(last, 3)
        store_dq(last, 3, 4)
        finish_dadj(last)
